import numpy as np
import ml_dtypes

BF16 = ml_dtypes.bfloat16


def bf(x):
    return np.asarray(x, np.float32).astype(BF16)


def f32(x):
    return np.asarray(x, np.float32)


def f64(x):
    return np.asarray(x).astype(np.float64)


def striped(idx):
    return np.tile(idx.reshape(-1, 16).T, (8, 1))


DIN, D, NC, C, S, N, H, K = 2048, 128, 8, 1024, 512, 4096, 256, 16


def setup_inputs():
    return {
        "x": bf(np.random.standard_normal((DIN, N))),
        "wp": bf(np.random.standard_normal((DIN, D)) / np.sqrt(DIN)),
        "bp": f32(0.1 * np.random.standard_normal((D, 1))),
        "ws": bf(np.random.standard_normal((DIN, D)) / np.sqrt(DIN)),
        "bs": f32(0.1 * np.random.standard_normal((D, 1))),
        "wc": bf(np.random.standard_normal((D, S)) / np.sqrt(D)),
        "bc": f32(0.1 * np.random.standard_normal((S, 1))),
        "cw": f32(0.25 * np.random.standard_normal((C, S))),
        "offs": striped(np.concatenate([np.random.permutation(S)[:H] for _ in range(K)])),
    }


def reference(x, wp, bp, ws, bs, wc, bc, cw, offs):
    idx = offs[:16].T.reshape(-1)
    hp = f64(wp).T @ f64(x) + f64(bp)
    lp = f64(wc).T @ hp + f64(bc)
    hs = f64(ws).T @ f64(x) + f64(bs)
    q = f64(cw)[:, idx] * np.tile(hs, (NC, 1))
    lc = q.reshape(NC, D, N).sum(axis=1)
    return np.concatenate([lp, lc, hp, hs], axis=0)

@@ -1,0 +1,121 @@
+import concourse.mybir as mybir
+
+FP32 = mybir.dt.float32
+BF16 = mybir.dt.bfloat16
+U16 = mybir.dt.uint16
+MULT = mybir.AluOpType.mult
+IDENTITY = mybir.ActivationFunctionType.Identity
+
+P = 128
+DIN, D, NCHILD, S, N = 2048, 128, 8, 512, 4096
+KC = DIN // P
+KG = 4
+BW = 512
+NB = N // BW
+SC = S // P
+QUAD = 32
+NT = P // QUAD
+ROWS = NCHILD * NB // NT
+
+ROW_LC, ROW_HP, ROW_HS = S, S + NCHILD, S + NCHILD + D
+
+FLOPS = 2 * DIN * 2 * D * N + 2 * D * S * N + 2 * NCHILD * D * N
+
+
+def tile_jointembeddingclassifier_b_kernel(tc, x, wp, bp, ws, bs, wc, bc, cw, offs, out):
+    nc = tc.nc
+    x_view = x.rearrange("(p k) j -> p k j", k=KC)
+    with (
+        tc.tile_pool(name="held", bufs=1) as held,
+        tc.tile_pool(name="xs", bufs=4) as xs,
+        tc.tile_pool(name="acts", bufs=3) as acts,
+        tc.tile_pool(name="prods", bufs=2) as prods,
+        tc.psum_pool(name="acc", bufs=2) as acc,
+        tc.psum_pool(name="lcacc", bufs=1) as lcacc,
+    ):
+        ws_sb = held.tile([P, KC, D], BF16, name="ws_sb")
+        nc.sync.dma_start(ws_sb[:], ws.rearrange("(p k) d -> p k d", k=KC))
+        wp_sb = held.tile([P, KC, D], BF16, name="wp_sb")
+        nc.scalar.dma_start(wp_sb[:], wp.rearrange("(p k) d -> p k d", k=KC))
+        offsets = held.tile([P, N // 16], U16, name="offsets")
+        nc.sync.dma_start(offsets[:], offs)
+        bs_sb = held.tile([P, 1], FP32, name="bs_sb")
+        nc.scalar.dma_start(bs_sb[:], bs)
+        bp_sb = held.tile([P, 1], FP32, name="bp_sb")
+        nc.scalar.dma_start(bp_sb[:], bp)
+        cw_sb = []
+        for n in range(NCHILD):
+            window = held.tile([P, S], FP32, name=f"cw{n}")
+            nc.scalar.dma_start(window[:], cw[n * P : (n + 1) * P, :])
+            cw_sb.append(window)
+        wc_sb = held.tile([P, S], BF16, name="wc_sb")
+        nc.scalar.dma_start(wc_sb[:], wc)
+        bc_sb = []
+        for c in range(SC):
+            bias = held.tile([P, 1], FP32, name=f"bc{c}")
+            nc.scalar.dma_start(bias[:], bc[c * P : (c + 1) * P, :])
+            bc_sb.append(bias)
+
+        strip = held.tile([P, QUAD + ROWS - 1], BF16, name="strip")
+        nc.vector.memset(strip[:], 0.0)
+        nc.vector.memset(strip[:, ROWS - 1 : ROWS], 1.0)
+
+        lc_ps = lcacc.tile([P, BW], FP32, name="lc_ps")
+
+        for b in range(NB):
+            cols = slice(b * BW, (b + 1) * BW)
+            x_sb = xs.tile([P, KC, BW], BF16, name="x_sb")
+            for g in range(KC // KG):
+                ks = slice(g * KG, (g + 1) * KG)
+                nc.sync.dma_start(x_sb[:, ks, :], x_view[:, ks, cols])
+
+            hs_ps = acc.tile([P, BW], FP32, name="hs_ps")
+            for k in range(KC):
+                nc.tensor.matmul(hs_ps[:], ws_sb[:, k, :], x_sb[:, k, :], start=(k == 0), stop=(k == KC - 1))
+            hs_sb = acts.tile([P, BW], FP32, name="hs_sb")
+            nc.scalar.activation(hs_sb[:], hs_ps[:], IDENTITY, bias=bs_sb[:])
+            nc.sync.dma_start(out[ROW_HS : ROW_HS + D, cols], hs_sb[:])
+
+            hp_ps = acc.tile([P, BW], FP32, name="hp_ps")
+            for k in range(KC):
+                nc.tensor.matmul(hp_ps[:], wp_sb[:, k, :], x_sb[:, k, :], start=(k == 0), stop=(k == KC - 1))
+            hp_bf = acts.tile([P, BW], BF16, name="hp_bf")
+            nc.scalar.activation(hp_bf[:], hp_ps[:], IDENTITY, bias=bp_sb[:])
+            hp_sb = acts.tile([P, BW], FP32, name="hp_sb")
+            nc.scalar.activation(hp_sb[:], hp_ps[:], IDENTITY, bias=bp_sb[:])
+            nc.sync.dma_start(out[ROW_HP : ROW_HP + D, cols], hp_sb[:])
+
+            lp_sb = acts.tile([P, SC, BW], FP32, name="lp_sb")
+            for c in range(SC):
+                lp_ps = acc.tile([P, BW], FP32, name="lp_ps")
+                nc.tensor.matmul(lp_ps[:], wc_sb[:, c * P : (c + 1) * P], hp_bf[:], start=True, stop=True)
+                nc.scalar.activation(lp_sb[:, c, :], lp_ps[:], IDENTITY, bias=bc_sb[c][:])
+            nc.sync.dma_start(out[0:S, cols].rearrange("(c p) j -> p c j", p=P), lp_sb[:])
+
+            block_offsets = offsets[:, b * (BW // 16) : (b + 1) * (BW // 16)]
+            q = prods.tile([P, NCHILD, BW], FP32, name="q")
+            q_bf = prods.tile([P, NCHILD, BW], BF16, name="q_bf")
+            for s in range(NCHILD // NT):
+                for t in range(NT):
+                    n = NT * s + t
+                    nc.vector.tensor_tensor(q[:, n, :], cw_sb[n][:].indirect(block_offsets), hs_sb[:], MULT)
+                four = slice(NT * s, NT * (s + 1))
+                nc.scalar.copy(q_bf[:, four, :], q[:, four, :])
+                r = NB * s + b
+                for t in range(NT):
+                    nc.tensor.matmul(
+                        lc_ps[QUAD * t : QUAD * (t + 1), :],
+                        strip[:, ROWS - 1 - r : ROWS - 1 - r + QUAD],
+                        q_bf[:, NT * s + t, :],
+                        start=(r == 0),
+                        stop=(r == ROWS - 1),
+                    )
+
+        lc_sb = held.tile([P, BW], FP32, name="lc_sb")
+        nc.scalar.copy(lc_sb[:], lc_ps[:])
+        for n in range(NCHILD):
+            first = QUAD * (n % NT) + NB * (n // NT)
+            nc.sync.dma_start(
+                out[ROW_LC + n : ROW_LC + n + 1, :].rearrange("o (b j) -> (o b) j", j=BW),
+                lc_sb[first : first + NB, :],
+            )

@@ -30,24 +30,37 @@ def tile_jointembeddingclassifier_b_kernel(tc, x, wp, bp, ws, bs, wc, bc, cw, of
         tc.tile_pool(name="xs", bufs=4) as xs,
         tc.tile_pool(name="acts", bufs=3) as acts,
         tc.tile_pool(name="prods", bufs=2) as prods,
-        tc.psum_pool(name="acc", bufs=2) as acc,
-        tc.psum_pool(name="lcacc", bufs=1) as lcacc,
+        tc.psum_pool(name="hs_acc", bufs=2) as hs_acc,
+        tc.psum_pool(name="hp_acc", bufs=1) as hp_acc,
+        tc.psum_pool(name="lp_acc", bufs=4) as lp_acc,
+        tc.psum_pool(name="lc_acc", bufs=1) as lc_acc,
     ):
+        x_sb = {}
+
+        def load_x(b):
+            x_sb[b] = xs.tile([P, KC, BW], BF16, name="x_sb")
+            for g in range(KC // KG):
+                ks = slice(g * KG, (g + 1) * KG)
+                nc.sync.dma_start(x_sb[b][:, ks, :], x_view[:, ks, b * BW : (b + 1) * BW])
+
         ws_sb = held.tile([P, KC, D], BF16, name="ws_sb")
         nc.sync.dma_start(ws_sb[:], ws.rearrange("(p k) d -> p k d", k=KC))
-        wp_sb = held.tile([P, KC, D], BF16, name="wp_sb")
-        nc.scalar.dma_start(wp_sb[:], wp.rearrange("(p k) d -> p k d", k=KC))
+        load_x(0)
         offsets = held.tile([P, N // 16], U16, name="offsets")
         nc.sync.dma_start(offsets[:], offs)
+        wp_sb = held.tile([P, KC, D], BF16, name="wp_sb")
+        nc.sync.dma_start(wp_sb[:], wp.rearrange("(p k) d -> p k d", k=KC))
+        cw_sb = []
+        for n in range(NCHILD):
+            window = held.tile([P, S], FP32, name=f"cw{n}")
+            nc.sync.dma_start(window[:], cw[n * P : (n + 1) * P, :])
+            cw_sb.append(window)
+        load_x(1)
+
         bs_sb = held.tile([P, 1], FP32, name="bs_sb")
         nc.scalar.dma_start(bs_sb[:], bs)
         bp_sb = held.tile([P, 1], FP32, name="bp_sb")
         nc.scalar.dma_start(bp_sb[:], bp)
-        cw_sb = []
-        for n in range(NCHILD):
-            window = held.tile([P, S], FP32, name=f"cw{n}")
-            nc.scalar.dma_start(window[:], cw[n * P : (n + 1) * P, :])
-            cw_sb.append(window)
         wc_sb = held.tile([P, S], BF16, name="wc_sb")
         nc.scalar.dma_start(wc_sb[:], wc)
         bc_sb = []
@@ -60,56 +73,72 @@ def tile_jointembeddingclassifier_b_kernel(tc, x, wp, bp, ws, bs, wc, bc, cw, of
         nc.vector.memset(strip[:], 0.0)
         nc.vector.memset(strip[:, ROWS - 1 : ROWS], 1.0)
 
-        lc_ps = lcacc.tile([P, BW], FP32, name="lc_ps")
+        lc_ps = lc_acc.tile([P, BW], FP32, name="lc_ps")
 
-        for b in range(NB):
+        hs_sb, hp_bf, q, q_bf = {}, {}, {}, {}
+
+        def project(acc_pool, name, w_sb, b):
+            ps = acc_pool.tile([P, BW], FP32, name=name)
+            for k in range(KC):
+                nc.tensor.matmul(ps[:], w_sb[:, k, :], x_sb[b][:, k, :], start=(k == 0), stop=(k == KC - 1))
+            return ps
+
+        def look_up(b, s):
+            block_offsets = offsets[:, b * (BW // 16) : (b + 1) * (BW // 16)]
+            for n in range(NT * s, NT * (s + 1)):
+                nc.vector.tensor_tensor(q[b][:, n, :], cw_sb[n][:].indirect(block_offsets), hs_sb[b][:], MULT)
+
+        def round_products(b, s):
+            four = slice(NT * s, NT * (s + 1))
+            nc.scalar.copy(q_bf[b][:, four, :], q[b][:, four, :])
+
+        def sum_products(b, s):
+            r = NB * s + b
+            for t in range(NT):
+                nc.tensor.matmul(
+                    lc_ps[QUAD * t : QUAD * (t + 1), :],
+                    strip[:, ROWS - 1 - r : ROWS - 1 - r + QUAD],
+                    q_bf[b][:, NT * s + t, :],
+                    start=(r == 0),
+                    stop=(r == ROWS - 1),
+                )
+
+        def parent_logits(b):
             cols = slice(b * BW, (b + 1) * BW)
-            x_sb = xs.tile([P, KC, BW], BF16, name="x_sb")
-            for g in range(KC // KG):
-                ks = slice(g * KG, (g + 1) * KG)
-                nc.sync.dma_start(x_sb[:, ks, :], x_view[:, ks, cols])
-
-            hs_ps = acc.tile([P, BW], FP32, name="hs_ps")
-            for k in range(KC):
-                nc.tensor.matmul(hs_ps[:], ws_sb[:, k, :], x_sb[:, k, :], start=(k == 0), stop=(k == KC - 1))
-            hs_sb = acts.tile([P, BW], FP32, name="hs_sb")
-            nc.scalar.activation(hs_sb[:], hs_ps[:], IDENTITY, bias=bs_sb[:])
-            nc.sync.dma_start(out[ROW_HS : ROW_HS + D, cols], hs_sb[:])
-
-            hp_ps = acc.tile([P, BW], FP32, name="hp_ps")
-            for k in range(KC):
-                nc.tensor.matmul(hp_ps[:], wp_sb[:, k, :], x_sb[:, k, :], start=(k == 0), stop=(k == KC - 1))
-            hp_bf = acts.tile([P, BW], BF16, name="hp_bf")
-            nc.scalar.activation(hp_bf[:], hp_ps[:], IDENTITY, bias=bp_sb[:])
-            hp_sb = acts.tile([P, BW], FP32, name="hp_sb")
-            nc.scalar.activation(hp_sb[:], hp_ps[:], IDENTITY, bias=bp_sb[:])
-            nc.sync.dma_start(out[ROW_HP : ROW_HP + D, cols], hp_sb[:])
-
             lp_sb = acts.tile([P, SC, BW], FP32, name="lp_sb")
             for c in range(SC):
-                lp_ps = acc.tile([P, BW], FP32, name="lp_ps")
-                nc.tensor.matmul(lp_ps[:], wc_sb[:, c * P : (c + 1) * P], hp_bf[:], start=True, stop=True)
+                lp_ps = lp_acc.tile([P, BW], FP32, name="lp_ps")
+                nc.tensor.matmul(lp_ps[:], wc_sb[:, c * P : (c + 1) * P], hp_bf[b][:], start=True, stop=True)
                 nc.scalar.activation(lp_sb[:, c, :], lp_ps[:], IDENTITY, bias=bc_sb[c][:])
             nc.sync.dma_start(out[0:S, cols].rearrange("(c p) j -> p c j", p=P), lp_sb[:])
 
-            block_offsets = offsets[:, b * (BW // 16) : (b + 1) * (BW // 16)]
-            q = prods.tile([P, NCHILD, BW], FP32, name="q")
-            q_bf = prods.tile([P, NCHILD, BW], BF16, name="q_bf")
-            for s in range(NCHILD // NT):
-                for t in range(NT):
-                    n = NT * s + t
-                    nc.vector.tensor_tensor(q[:, n, :], cw_sb[n][:].indirect(block_offsets), hs_sb[:], MULT)
-                four = slice(NT * s, NT * (s + 1))
-                nc.scalar.copy(q_bf[:, four, :], q[:, four, :])
-                r = NB * s + b
-                for t in range(NT):
-                    nc.tensor.matmul(
-                        lc_ps[QUAD * t : QUAD * (t + 1), :],
-                        strip[:, ROWS - 1 - r : ROWS - 1 - r + QUAD],
-                        q_bf[:, NT * s + t, :],
-                        start=(r == 0),
-                        stop=(r == ROWS - 1),
-                    )
+        for b in range(NB + 1):
+            cols = slice(b * BW, (b + 1) * BW)
+            if b + 2 < NB:
+                load_x(b + 2)
+            if b < NB:
+                hs_ps = project(hs_acc, "hs_ps", ws_sb, b)
+                hs_sb[b] = acts.tile([P, BW], FP32, name="hs_sb")
+                nc.scalar.activation(hs_sb[b][:], hs_ps[:], IDENTITY, bias=bs_sb[:])
+                nc.sync.dma_start(out[ROW_HS : ROW_HS + D, cols], hs_sb[b][:])
+            if b > 0:
+                round_products(b - 1, 1)
+                parent_logits(b - 1)
+            if b < NB:
+                q[b] = prods.tile([P, NCHILD, BW], FP32, name="q")
+                q_bf[b] = prods.tile([P, NCHILD, BW], BF16, name="q_bf")
+                look_up(b, 0)
+                round_products(b, 0)
+                look_up(b, 1)
+                hp_ps = project(hp_acc, "hp_ps", wp_sb, b)
+                hp_bf[b] = acts.tile([P, BW], BF16, name="hp_bf")
+                nc.scalar.activation(hp_bf[b][:], hp_ps[:], IDENTITY, bias=bp_sb[:])
+                hp_sb = acts.tile([P, BW], FP32, name="hp_sb")
+                nc.scalar.activation(hp_sb[:], hp_ps[:], IDENTITY, bias=bp_sb[:])
+                nc.sync.dma_start(out[ROW_HP : ROW_HP + D, cols], hp_sb[:])
+            if b > 0:
+                sum_products(b - 1, 0)
+                sum_products(b - 1, 1)
 
         lc_sb = held.tile([P, BW], FP32, name="lc_sb")
         nc.scalar.copy(lc_sb[:], lc_ps[:])

@@ -13,9 +13,8 @@ KG = 4
 BW = 512
 NB = N // BW
 SC = S // P
-QUAD = 32
-NT = P // QUAD
-ROWS = NCHILD * NB // NT
+NT = 4
+LAST = NCHILD * NB - 1
 
 ROW_LC, ROW_HP, ROW_HS = S, S + NCHILD, S + NCHILD + D
 
@@ -69,9 +68,9 @@ def tile_jointembeddingclassifier_b_kernel(tc, x, wp, bp, ws, bs, wc, bc, cw, of
             nc.scalar.dma_start(bias[:], bc[c * P : (c + 1) * P, :])
             bc_sb.append(bias)
 
-        strip = held.tile([P, QUAD + ROWS - 1], BF16, name="strip")
+        strip = held.tile([P, P + LAST], BF16, name="strip")
         nc.vector.memset(strip[:], 0.0)
-        nc.vector.memset(strip[:, ROWS - 1 : ROWS], 1.0)
+        nc.vector.memset(strip[:, LAST : LAST + 1], 1.0)
 
         lc_ps = lc_acc.tile([P, BW], FP32, name="lc_ps")
 
@@ -93,14 +92,14 @@ def tile_jointembeddingclassifier_b_kernel(tc, x, wp, bp, ws, bs, wc, bc, cw, of
             nc.scalar.copy(q_bf[b][:, four, :], q[b][:, four, :])
 
         def sum_products(b, s):
-            r = NB * s + b
-            for t in range(NT):
+            for n in range(NT * s, NT * (s + 1)):
+                r = NB * n + b
                 nc.tensor.matmul(
-                    lc_ps[QUAD * t : QUAD * (t + 1), :],
-                    strip[:, ROWS - 1 - r : ROWS - 1 - r + QUAD],
-                    q_bf[b][:, NT * s + t, :],
+                    lc_ps[:],
+                    strip[:, LAST - r : LAST - r + P],
+                    q_bf[b][:, n, :],
                     start=(r == 0),
-                    stop=(r == ROWS - 1),
+                    stop=(r == LAST),
                 )
 
         def parent_logits(b):
@@ -143,7 +142,7 @@ def tile_jointembeddingclassifier_b_kernel(tc, x, wp, bp, ws, bs, wc, bc, cw, of
         lc_sb = held.tile([P, BW], FP32, name="lc_sb")
         nc.scalar.copy(lc_sb[:], lc_ps[:])
         for n in range(NCHILD):
-            first = QUAD * (n % NT) + NB * (n // NT)
+            first = NB * n
             nc.sync.dma_start(
                 out[ROW_LC + n : ROW_LC + n + 1, :].rearrange("o (b j) -> (o b) j", j=BW),
                 lc_sb[first : first + NB, :],

@@ -13,8 +13,9 @@ KG = 4
 BW = 512
 NB = N // BW
 SC = S // P
-NT = 4
-LAST = NCHILD * NB - 1
+QUAD = 32
+NT = P // QUAD
+ROWS = NCHILD * NB // NT
 
 ROW_LC, ROW_HP, ROW_HS = S, S + NCHILD, S + NCHILD + D
 
@@ -68,9 +69,9 @@ def tile_jointembeddingclassifier_b_kernel(tc, x, wp, bp, ws, bs, wc, bc, cw, of
             nc.scalar.dma_start(bias[:], bc[c * P : (c + 1) * P, :])
             bc_sb.append(bias)
 
-        strip = held.tile([P, P + LAST], BF16, name="strip")
+        strip = held.tile([P, QUAD + ROWS - 1], BF16, name="strip")
         nc.vector.memset(strip[:], 0.0)
-        nc.vector.memset(strip[:, LAST : LAST + 1], 1.0)
+        nc.vector.memset(strip[:, ROWS - 1 : ROWS], 1.0)
 
         lc_ps = lc_acc.tile([P, BW], FP32, name="lc_ps")
 
@@ -87,19 +88,19 @@ def tile_jointembeddingclassifier_b_kernel(tc, x, wp, bp, ws, bs, wc, bc, cw, of
             for n in range(NT * s, NT * (s + 1)):
                 nc.vector.tensor_tensor(q[b][:, n, :], cw_sb[n][:].indirect(block_offsets), hs_sb[b][:], MULT)
 
-        def round_products(b, s):
+        def round_products(engine_copy, b, s):
             four = slice(NT * s, NT * (s + 1))
-            nc.scalar.copy(q_bf[b][:, four, :], q[b][:, four, :])
+            engine_copy(q_bf[b][:, four, :], q[b][:, four, :])
 
         def sum_products(b, s):
-            for n in range(NT * s, NT * (s + 1)):
-                r = NB * n + b
+            r = NB * s + b
+            for t in range(NT):
                 nc.tensor.matmul(
-                    lc_ps[:],
-                    strip[:, LAST - r : LAST - r + P],
-                    q_bf[b][:, n, :],
+                    lc_ps[QUAD * t : QUAD * (t + 1), :],
+                    strip[:, ROWS - 1 - r : ROWS - 1 - r + QUAD],
+                    q_bf[b][:, NT * s + t, :],
                     start=(r == 0),
-                    stop=(r == LAST),
+                    stop=(r == ROWS - 1),
                 )
 
         def parent_logits(b):
@@ -121,14 +122,14 @@ def tile_jointembeddingclassifier_b_kernel(tc, x, wp, bp, ws, bs, wc, bc, cw, of
                 nc.scalar.activation(hs_sb[b][:], hs_ps[:], IDENTITY, bias=bs_sb[:])
                 nc.sync.dma_start(out[ROW_HS : ROW_HS + D, cols], hs_sb[b][:])
             if b > 0:
-                round_products(b - 1, 1)
                 parent_logits(b - 1)
             if b < NB:
                 q[b] = prods.tile([P, NCHILD, BW], FP32, name="q")
                 q_bf[b] = prods.tile([P, NCHILD, BW], BF16, name="q_bf")
                 look_up(b, 0)
-                round_products(b, 0)
+                round_products(nc.scalar.copy, b, 0)
                 look_up(b, 1)
+                round_products(nc.vector.tensor_copy, b, 1)
                 hp_ps = project(hp_acc, "hp_ps", wp_sb, b)
                 hp_bf[b] = acts.tile([P, BW], BF16, name="hp_bf")
                 nc.scalar.activation(hp_bf[b][:], hp_ps[:], IDENTITY, bias=bp_sb[:])
@@ -142,7 +143,7 @@ def tile_jointembeddingclassifier_b_kernel(tc, x, wp, bp, ws, bs, wc, bc, cw, of
         lc_sb = held.tile([P, BW], FP32, name="lc_sb")
         nc.scalar.copy(lc_sb[:], lc_ps[:])
         for n in range(NCHILD):
-            first = NB * n
+            first = QUAD * (n % NT) + NB * (n // NT)
             nc.sync.dma_start(
                 out[ROW_LC + n : ROW_LC + n + 1, :].rearrange("o (b j) -> (o b) j", j=BW),
                 lc_sb[first : first + NB, :],

@@ -37,11 +37,14 @@ def tile_jointembeddingclassifier_b_kernel(tc, x, wp, bp, ws, bs, wc, bc, cw, of
     ):
         x_sb = {}
 
+        def load_x_piece(b, g):
+            ks = slice(g * KG, (g + 1) * KG)
+            nc.sync.dma_start(x_sb[b][:, ks, :], x_view[:, ks, b * BW : (b + 1) * BW])
+
         def load_x(b):
             x_sb[b] = xs.tile([P, KC, BW], BF16, name="x_sb")
             for g in range(KC // KG):
-                ks = slice(g * KG, (g + 1) * KG)
-                nc.sync.dma_start(x_sb[b][:, ks, :], x_view[:, ks, b * BW : (b + 1) * BW])
+                load_x_piece(b, g)
 
         ws_sb = held.tile([P, KC, D], BF16, name="ws_sb")
         nc.sync.dma_start(ws_sb[:], ws.rearrange("(p k) d -> p k d", k=KC))
@@ -50,12 +53,17 @@ def tile_jointembeddingclassifier_b_kernel(tc, x, wp, bp, ws, bs, wc, bc, cw, of
         nc.sync.dma_start(offsets[:], offs)
         wp_sb = held.tile([P, KC, D], BF16, name="wp_sb")
         nc.sync.dma_start(wp_sb[:], wp.rearrange("(p k) d -> p k d", k=KC))
-        cw_sb = []
-        for n in range(NCHILD):
-            window = held.tile([P, S], FP32, name=f"cw{n}")
-            nc.sync.dma_start(window[:], cw[n * P : (n + 1) * P, :])
-            cw_sb.append(window)
-        load_x(1)
+        cw_sb = [held.tile([P, S], FP32, name=f"cw{n}") for n in range(NCHILD)]
+
+        def load_cw(n):
+            nc.sync.dma_start(cw_sb[n][:], cw[n * P : (n + 1) * P, :])
+
+        for n in range(NCHILD // 2):
+            load_cw(n)
+        x_sb[1] = xs.tile([P, KC, BW], BF16, name="x_sb")
+        for g in range(KC // KG):
+            load_x_piece(1, g)
+            load_cw(NCHILD // 2 + g)
 
         bs_sb = held.tile([P, 1], FP32, name="bs_sb")
         nc.scalar.dma_start(bs_sb[:], bs)
@@ -83,14 +91,13 @@ def tile_jointembeddingclassifier_b_kernel(tc, x, wp, bp, ws, bs, wc, bc, cw, of
                 nc.tensor.matmul(ps[:], w_sb[:, k, :], x_sb[b][:, k, :], start=(k == 0), stop=(k == KC - 1))
             return ps
 
-        def look_up(b, s):
+        def look_up(b, first, last):
             block_offsets = offsets[:, b * (BW // 16) : (b + 1) * (BW // 16)]
-            for n in range(NT * s, NT * (s + 1)):
+            for n in range(first, last):
                 nc.vector.tensor_tensor(q[b][:, n, :], cw_sb[n][:].indirect(block_offsets), hs_sb[b][:], MULT)
 
-        def round_products(engine_copy, b, s):
-            four = slice(NT * s, NT * (s + 1))
-            engine_copy(q_bf[b][:, four, :], q[b][:, four, :])
+        def round_products(engine_copy, b, first, last):
+            engine_copy(q_bf[b][:, first:last, :], q[b][:, first:last, :])
 
         def sum_products(b, s):
             r = NB * s + b
@@ -126,10 +133,12 @@ def tile_jointembeddingclassifier_b_kernel(tc, x, wp, bp, ws, bs, wc, bc, cw, of
             if b < NB:
                 q[b] = prods.tile([P, NCHILD, BW], FP32, name="q")
                 q_bf[b] = prods.tile([P, NCHILD, BW], BF16, name="q_bf")
-                look_up(b, 0)
-                round_products(nc.scalar.copy, b, 0)
-                look_up(b, 1)
-                round_products(nc.vector.tensor_copy, b, 1)
+                look_up(b, 0, 2)
+                round_products(nc.scalar.copy, b, 0, 2)
+                look_up(b, 2, 4)
+                round_products(nc.scalar.copy, b, 2, 4)
+                look_up(b, 4, 8)
+                round_products(nc.vector.tensor_copy, b, 4, 8)
                 hp_ps = project(hp_acc, "hp_ps", wp_sb, b)
                 hp_bf[b] = acts.tile([P, BW], BF16, name="hp_bf")
                 nc.scalar.activation(hp_bf[b][:], hp_ps[:], IDENTITY, bias=bp_sb[:])

@@ -13,9 +13,8 @@ KG = 4
 BW = 512
 NB = N // BW
 SC = S // P
-QUAD = 32
-NT = P // QUAD
-ROWS = NCHILD * NB // NT
+NT = 4
+LAST = NCHILD * NB - 1
 
 ROW_LC, ROW_HP, ROW_HS = S, S + NCHILD, S + NCHILD + D
 
@@ -77,9 +76,9 @@ def tile_jointembeddingclassifier_b_kernel(tc, x, wp, bp, ws, bs, wc, bc, cw, of
             nc.scalar.dma_start(bias[:], bc[c * P : (c + 1) * P, :])
             bc_sb.append(bias)
 
-        strip = held.tile([P, QUAD + ROWS - 1], BF16, name="strip")
+        strip = held.tile([P, P + LAST], BF16, name="strip")
         nc.vector.memset(strip[:], 0.0)
-        nc.vector.memset(strip[:, ROWS - 1 : ROWS], 1.0)
+        nc.vector.memset(strip[:, LAST : LAST + 1], 1.0)
 
         lc_ps = lc_acc.tile([P, BW], FP32, name="lc_ps")
 
@@ -100,14 +99,14 @@ def tile_jointembeddingclassifier_b_kernel(tc, x, wp, bp, ws, bs, wc, bc, cw, of
             engine_copy(q_bf[b][:, first:last, :], q[b][:, first:last, :])
 
         def sum_products(b, s):
-            r = NB * s + b
-            for t in range(NT):
+            for n in range(NT * s, NT * (s + 1)):
+                r = NB * n + b
                 nc.tensor.matmul(
-                    lc_ps[QUAD * t : QUAD * (t + 1), :],
-                    strip[:, ROWS - 1 - r : ROWS - 1 - r + QUAD],
-                    q_bf[b][:, NT * s + t, :],
+                    lc_ps[:],
+                    strip[:, LAST - r : LAST - r + P],
+                    q_bf[b][:, n, :],
                     start=(r == 0),
-                    stop=(r == ROWS - 1),
+                    stop=(r == LAST),
                 )
 
         def parent_logits(b):
@@ -152,7 +151,7 @@ def tile_jointembeddingclassifier_b_kernel(tc, x, wp, bp, ws, bs, wc, bc, cw, of
         lc_sb = held.tile([P, BW], FP32, name="lc_sb")
         nc.scalar.copy(lc_sb[:], lc_ps[:])
         for n in range(NCHILD):
-            first = QUAD * (n % NT) + NB * (n // NT)
+            first = NB * n
             nc.sync.dma_start(
                 out[ROW_LC + n : ROW_LC + n + 1, :].rearrange("o (b j) -> (o b) j", j=BW),
                 lc_sb[first : first + NB, :],

@@ -13,8 +13,9 @@ KG = 4
 BW = 512
 NB = N // BW
 SC = S // P
-NT = 4
-LAST = NCHILD * NB - 1
+QUAD = 32
+NT = P // QUAD
+ROWS = NCHILD * NB // NT
 
 ROW_LC, ROW_HP, ROW_HS = S, S + NCHILD, S + NCHILD + D
 
@@ -28,6 +29,7 @@ def tile_jointembeddingclassifier_b_kernel(tc, x, wp, bp, ws, bs, wc, bc, cw, of
         tc.tile_pool(name="held", bufs=1) as held,
         tc.tile_pool(name="xs", bufs=4) as xs,
         tc.tile_pool(name="acts", bufs=3) as acts,
+        tc.tile_pool(name="lps", bufs=8) as lps,
         tc.tile_pool(name="prods", bufs=2) as prods,
         tc.psum_pool(name="hs_acc", bufs=2) as hs_acc,
         tc.psum_pool(name="hp_acc", bufs=1) as hp_acc,
@@ -76,9 +78,9 @@ def tile_jointembeddingclassifier_b_kernel(tc, x, wp, bp, ws, bs, wc, bc, cw, of
             nc.scalar.dma_start(bias[:], bc[c * P : (c + 1) * P, :])
             bc_sb.append(bias)
 
-        strip = held.tile([P, P + LAST], BF16, name="strip")
+        strip = held.tile([P, QUAD + ROWS - 1], BF16, name="strip")
         nc.vector.memset(strip[:], 0.0)
-        nc.vector.memset(strip[:, LAST : LAST + 1], 1.0)
+        nc.vector.memset(strip[:, ROWS - 1 : ROWS], 1.0)
 
         lc_ps = lc_acc.tile([P, BW], FP32, name="lc_ps")
 
@@ -99,24 +101,24 @@ def tile_jointembeddingclassifier_b_kernel(tc, x, wp, bp, ws, bs, wc, bc, cw, of
             engine_copy(q_bf[b][:, first:last, :], q[b][:, first:last, :])
 
         def sum_products(b, s):
-            for n in range(NT * s, NT * (s + 1)):
-                r = NB * n + b
+            r = NB * s + b
+            for t in range(NT):
                 nc.tensor.matmul(
-                    lc_ps[:],
-                    strip[:, LAST - r : LAST - r + P],
-                    q_bf[b][:, n, :],
+                    lc_ps[QUAD * t : QUAD * (t + 1), :],
+                    strip[:, ROWS - 1 - r : ROWS - 1 - r + QUAD],
+                    q_bf[b][:, NT * s + t, :],
                     start=(r == 0),
-                    stop=(r == LAST),
+                    stop=(r == ROWS - 1),
                 )
 
         def parent_logits(b):
             cols = slice(b * BW, (b + 1) * BW)
-            lp_sb = acts.tile([P, SC, BW], FP32, name="lp_sb")
             for c in range(SC):
                 lp_ps = lp_acc.tile([P, BW], FP32, name="lp_ps")
                 nc.tensor.matmul(lp_ps[:], wc_sb[:, c * P : (c + 1) * P], hp_bf[b][:], start=True, stop=True)
-                nc.scalar.activation(lp_sb[:, c, :], lp_ps[:], IDENTITY, bias=bc_sb[c][:])
-            nc.sync.dma_start(out[0:S, cols].rearrange("(c p) j -> p c j", p=P), lp_sb[:])
+                lp_sb = lps.tile([P, BW], FP32, name="lp_sb")
+                nc.scalar.activation(lp_sb[:], lp_ps[:], IDENTITY, bias=bc_sb[c][:])
+                nc.sync.dma_start(out[c * P : (c + 1) * P, cols], lp_sb[:])
 
         for b in range(NB + 1):
             cols = slice(b * BW, (b + 1) * BW)
@@ -136,8 +138,10 @@ def tile_jointembeddingclassifier_b_kernel(tc, x, wp, bp, ws, bs, wc, bc, cw, of
                 round_products(nc.scalar.copy, b, 0, 2)
                 look_up(b, 2, 4)
                 round_products(nc.scalar.copy, b, 2, 4)
-                look_up(b, 4, 8)
-                round_products(nc.vector.tensor_copy, b, 4, 8)
+                look_up(b, 4, 6)
+                round_products(nc.scalar.copy, b, 4, 6)
+                look_up(b, 6, 8)
+                round_products(nc.vector.tensor_copy, b, 6, 8)
                 hp_ps = project(hp_acc, "hp_ps", wp_sb, b)
                 hp_bf[b] = acts.tile([P, BW], BF16, name="hp_bf")
                 nc.scalar.activation(hp_bf[b][:], hp_ps[:], IDENTITY, bias=bp_sb[:])
@@ -151,7 +155,7 @@ def tile_jointembeddingclassifier_b_kernel(tc, x, wp, bp, ws, bs, wc, bc, cw, of
         lc_sb = held.tile([P, BW], FP32, name="lc_sb")
         nc.scalar.copy(lc_sb[:], lc_ps[:])
         for n in range(NCHILD):
-            first = NB * n
+            first = QUAD * (n % NT) + NB * (n // NT)
             nc.sync.dma_start(
                 out[ROW_LC + n : ROW_LC + n + 1, :].rearrange("o (b j) -> (o b) j", j=BW),
                 lc_sb[first : first + NB, :],

@@ -12,6 +12,7 @@ KC = DIN // P
 KG = 4
 BW = 512
 NB = N // BW
+LAST = NB - 1
 SC = S // P
 QUAD = 32
 NT = P // QUAD
@@ -31,6 +32,7 @@ def tile_jointembeddingclassifier_b_kernel(tc, x, wp, bp, ws, bs, wc, bc, cw, of
         tc.tile_pool(name="acts", bufs=3) as acts,
         tc.tile_pool(name="lps", bufs=8) as lps,
         tc.tile_pool(name="prods", bufs=2) as prods,
+        tc.tile_pool(name="rounded", bufs=1) as rounded,
         tc.psum_pool(name="hs_acc", bufs=2) as hs_acc,
         tc.psum_pool(name="hp_acc", bufs=1) as hp_acc,
         tc.psum_pool(name="lp_acc", bufs=4) as lp_acc,
@@ -92,13 +94,32 @@ def tile_jointembeddingclassifier_b_kernel(tc, x, wp, bp, ws, bs, wc, bc, cw, of
                 nc.tensor.matmul(ps[:], w_sb[:, k, :], x_sb[b][:, k, :], start=(k == 0), stop=(k == KC - 1))
             return ps
 
-        def look_up(b, first, last):
+        def child_projection(b):
+            cols = slice(b * BW, (b + 1) * BW)
+            hs_ps = project(hs_acc, "hs_ps", ws_sb, b)
+            hs_sb[b] = acts.tile([P, BW], FP32, name="hs_sb")
+            nc.scalar.activation(hs_sb[b][:], hs_ps[:], IDENTITY, bias=bs_sb[:])
+            nc.sync.dma_start(out[ROW_HS : ROW_HS + D, cols], hs_sb[b][:])
+
+        def parent_projection(b):
+            cols = slice(b * BW, (b + 1) * BW)
+            hp_ps = project(hp_acc, "hp_ps", wp_sb, b)
+            hp_bf[b] = acts.tile([P, BW], BF16, name="hp_bf")
+            nc.scalar.activation(hp_bf[b][:], hp_ps[:], IDENTITY, bias=bp_sb[:])
+            hp_sb = acts.tile([P, BW], FP32, name="hp_sb")
+            nc.scalar.activation(hp_sb[:], hp_ps[:], IDENTITY, bias=bp_sb[:])
+            nc.sync.dma_start(out[ROW_HP : ROW_HP + D, cols], hp_sb[:])
+
+        def look_up(b):
+            q[b] = prods.tile([P, NCHILD, BW], FP32, name="q")
             block_offsets = offsets[:, b * (BW // 16) : (b + 1) * (BW // 16)]
-            for n in range(first, last):
+            for n in range(NCHILD):
                 nc.vector.tensor_tensor(q[b][:, n, :], cw_sb[n][:].indirect(block_offsets), hs_sb[b][:], MULT)
 
-        def round_products(engine_copy, b, first, last):
-            engine_copy(q_bf[b][:, first:last, :], q[b][:, first:last, :])
+        def round_products(engine_copy, name, b, s):
+            q_bf[b, s] = rounded.tile([P, NT, BW], BF16, name=name)
+            for t in range(0, NT, 2):
+                engine_copy(q_bf[b, s][:, t : t + 2, :], q[b][:, NT * s + t : NT * s + t + 2, :])
 
         def sum_products(b, s):
             r = NB * s + b
@@ -106,7 +127,7 @@ def tile_jointembeddingclassifier_b_kernel(tc, x, wp, bp, ws, bs, wc, bc, cw, of
                 nc.tensor.matmul(
                     lc_ps[QUAD * t : QUAD * (t + 1), :],
                     strip[:, ROWS - 1 - r : ROWS - 1 - r + QUAD],
-                    q_bf[b][:, NT * s + t, :],
+                    q_bf[b, s][:, t, :],
                     start=(r == 0),
                     stop=(r == ROWS - 1),
                 )
@@ -117,40 +138,34 @@ def tile_jointembeddingclassifier_b_kernel(tc, x, wp, bp, ws, bs, wc, bc, cw, of
                 lp_ps = lp_acc.tile([P, BW], FP32, name="lp_ps")
                 nc.tensor.matmul(lp_ps[:], wc_sb[:, c * P : (c + 1) * P], hp_bf[b][:], start=True, stop=True)
                 lp_sb = lps.tile([P, BW], FP32, name="lp_sb")
-                nc.scalar.activation(lp_sb[:], lp_ps[:], IDENTITY, bias=bc_sb[c][:])
+                if b == LAST and c % 2 == 1:
+                    nc.vector.tensor_scalar_add(lp_sb[:], lp_ps[:], bc_sb[c][:])
+                else:
+                    nc.scalar.activation(lp_sb[:], lp_ps[:], IDENTITY, bias=bc_sb[c][:])
                 nc.sync.dma_start(out[c * P : (c + 1) * P, cols], lp_sb[:])
 
-        for b in range(NB + 1):
-            cols = slice(b * BW, (b + 1) * BW)
-            if b + 2 < NB:
-                load_x(b + 2)
-            if b < NB:
-                hs_ps = project(hs_acc, "hs_ps", ws_sb, b)
-                hs_sb[b] = acts.tile([P, BW], FP32, name="hs_sb")
-                nc.scalar.activation(hs_sb[b][:], hs_ps[:], IDENTITY, bias=bs_sb[:])
-                nc.sync.dma_start(out[ROW_HS : ROW_HS + D, cols], hs_sb[b][:])
-            if b > 0:
-                parent_logits(b - 1)
-            if b < NB:
-                q[b] = prods.tile([P, NCHILD, BW], FP32, name="q")
-                q_bf[b] = prods.tile([P, NCHILD, BW], BF16, name="q_bf")
-                look_up(b, 0, 2)
-                round_products(nc.scalar.copy, b, 0, 2)
-                look_up(b, 2, 4)
-                round_products(nc.scalar.copy, b, 2, 4)
-                look_up(b, 4, 6)
-                round_products(nc.scalar.copy, b, 4, 6)
-                look_up(b, 6, 8)
-                round_products(nc.vector.tensor_copy, b, 6, 8)
-                hp_ps = project(hp_acc, "hp_ps", wp_sb, b)
-                hp_bf[b] = acts.tile([P, BW], BF16, name="hp_bf")
-                nc.scalar.activation(hp_bf[b][:], hp_ps[:], IDENTITY, bias=bp_sb[:])
-                hp_sb = acts.tile([P, BW], FP32, name="hp_sb")
-                nc.scalar.activation(hp_sb[:], hp_ps[:], IDENTITY, bias=bp_sb[:])
-                nc.sync.dma_start(out[ROW_HP : ROW_HP + D, cols], hp_sb[:])
-            if b > 0:
-                sum_products(b - 1, 0)
-                sum_products(b - 1, 1)
+        for i in range(NB + 2):
+            if i + 2 < NB:
+                load_x(i + 2)
+            if i < NB:
+                child_projection(i)
+            if 2 <= i:
+                sum_products(i - 2, 0)
+            if 1 <= i <= LAST:
+                round_products(nc.scalar.copy, "q_bf_lower", i - 1, 0)
+            if 2 <= i:
+                parent_logits(i - 2)
+            if i < NB:
+                look_up(i)
+            if i == LAST:
+                round_products(nc.vector.tensor_copy, "q_bf_lower_last", LAST, 0)
+                round_products(nc.vector.tensor_copy, "q_bf_upper_last", LAST, 1)
+            if 1 <= i <= NB:
+                parent_projection(i - 1)
+            if 2 <= i:
+                sum_products(i - 2, 1)
+            if 1 <= i <= LAST:
+                round_products(nc.scalar.copy, "q_bf_upper", i - 1, 1)
 
         lc_sb = held.tile([P, BW], FP32, name="lc_sb")
         nc.scalar.copy(lc_sb[:], lc_ps[:])

@@ -16,7 +16,8 @@ LAST = NB - 1
 SC = S // P
 QUAD = 32
 NT = P // QUAD
-ROWS = NCHILD * NB // NT
+HW = N * NCHILD // P
+NH = N // HW
 
 ROW_LC, ROW_HP, ROW_HS = S, S + NCHILD, S + NCHILD + D
 
@@ -58,15 +59,18 @@ def tile_jointembeddingclassifier_b_kernel(tc, x, wp, bp, ws, bs, wc, bc, cw, of
         nc.sync.dma_start(wp_sb[:], wp.rearrange("(p k) d -> p k d", k=KC))
         cw_sb = [held.tile([P, S], FP32, name=f"cw{n}") for n in range(NCHILD)]
 
+        def child_of(m):
+            return 2 * (m % NT) + m // NT
+
         def load_cw(n):
             nc.sync.dma_start(cw_sb[n][:], cw[n * P : (n + 1) * P, :])
 
-        for n in range(NCHILD // 2):
-            load_cw(n)
+        for m in range(NCHILD // 2):
+            load_cw(child_of(m))
         x_sb[1] = xs.tile([P, KC, BW], BF16, name="x_sb")
         for g in range(KC // KG):
             load_x_piece(1, g)
-            load_cw(NCHILD // 2 + g)
+            load_cw(child_of(NCHILD // 2 + g))
 
         bs_sb = held.tile([P, 1], FP32, name="bs_sb")
         nc.scalar.dma_start(bs_sb[:], bs)
@@ -80,11 +84,11 @@ def tile_jointembeddingclassifier_b_kernel(tc, x, wp, bp, ws, bs, wc, bc, cw, of
             nc.scalar.dma_start(bias[:], bc[c * P : (c + 1) * P, :])
             bc_sb.append(bias)
 
-        strip = held.tile([P, QUAD + ROWS - 1], BF16, name="strip")
+        strip = held.tile([P, 2 * QUAD - 1], BF16, name="strip")
         nc.vector.memset(strip[:], 0.0)
-        nc.vector.memset(strip[:, ROWS - 1 : ROWS], 1.0)
+        nc.vector.memset(strip[:, QUAD - 1 : QUAD], 1.0)
 
-        lc_ps = lc_acc.tile([P, BW], FP32, name="lc_ps")
+        lc_ps = lc_acc.tile([P, HW], FP32, name="lc_ps")
 
         hs_sb, hp_bf, q, q_bf = {}, {}, {}, {}
 
@@ -113,8 +117,9 @@ def tile_jointembeddingclassifier_b_kernel(tc, x, wp, bp, ws, bs, wc, bc, cw, of
         def look_up(b):
             q[b] = prods.tile([P, NCHILD, BW], FP32, name="q")
             block_offsets = offsets[:, b * (BW // 16) : (b + 1) * (BW // 16)]
-            for n in range(NCHILD):
-                nc.vector.tensor_tensor(q[b][:, n, :], cw_sb[n][:].indirect(block_offsets), hs_sb[b][:], MULT)
+            for m in range(NCHILD):
+                window = cw_sb[child_of(m)]
+                nc.vector.tensor_tensor(q[b][:, m, :], window[:].indirect(block_offsets), hs_sb[b][:], MULT)
 
         def round_products(engine_copy, name, b, s):
             q_bf[b, s] = rounded.tile([P, NT, BW], BF16, name=name)
@@ -122,15 +127,17 @@ def tile_jointembeddingclassifier_b_kernel(tc, x, wp, bp, ws, bs, wc, bc, cw, of
                 engine_copy(q_bf[b, s][:, t : t + 2, :], q[b][:, NT * s + t : NT * s + t + 2, :])
 
         def sum_products(b, s):
-            r = NB * s + b
-            for t in range(NT):
-                nc.tensor.matmul(
-                    lc_ps[QUAD * t : QUAD * (t + 1), :],
-                    strip[:, ROWS - 1 - r : ROWS - 1 - r + QUAD],
-                    q_bf[b, s][:, t, :],
-                    start=(r == 0),
-                    stop=(r == ROWS - 1),
-                )
+            for h in range(b * BW // HW, (b + 1) * BW // HW):
+                r = NH * s + h
+                first = h * HW - b * BW
+                for t in range(NT):
+                    nc.tensor.matmul(
+                        lc_ps[QUAD * t : QUAD * (t + 1), :],
+                        strip[:, QUAD - 1 - r : 2 * QUAD - 1 - r],
+                        q_bf[b, s][:, t, first : first + HW],
+                        start=(r == 0),
+                        stop=(r == QUAD - 1),
+                    )
 
         def parent_logits(b):
             cols = slice(b * BW, (b + 1) * BW)
@@ -167,11 +174,6 @@ def tile_jointembeddingclassifier_b_kernel(tc, x, wp, bp, ws, bs, wc, bc, cw, of
             if 1 <= i <= LAST:
                 round_products(nc.scalar.copy, "q_bf_upper", i - 1, 1)
 
-        lc_sb = held.tile([P, BW], FP32, name="lc_sb")
+        lc_sb = held.tile([P, HW], FP32, name="lc_sb")
         nc.scalar.copy(lc_sb[:], lc_ps[:])
-        for n in range(NCHILD):
-            first = QUAD * (n % NT) + NB * (n // NT)
-            nc.sync.dma_start(
-                out[ROW_LC + n : ROW_LC + n + 1, :].rearrange("o (b j) -> (o b) j", j=BW),
-                lc_sb[first : first + NB, :],
-            )
+        nc.sync.dma_start(out[ROW_LC : ROW_LC + NCHILD, :].rearrange("n (h j) -> (n h) j", j=HW), lc_sb[:])

@@ -11,13 +11,15 @@ DIN, D, NCHILD, S, N = 2048, 128, 8, 512, 4096
 KC = DIN // P
 KG = 4
 BW = 512
-NB = N // BW
-LAST = NB - 1
 SC = S // P
 QUAD = 32
 NT = P // QUAD
 HW = N * NCHILD // P
 NH = N // HW
+WIDTHS = [BW] * (N // BW - 1) + [HW, HW]
+FIRST = [sum(WIDTHS[:b]) for b in range(len(WIDTHS))]
+NB = len(WIDTHS)
+LAST = NB - 1
 
 ROW_LC, ROW_HP, ROW_HS = S, S + NCHILD, S + NCHILD + D
 
@@ -41,12 +43,15 @@ def tile_jointembeddingclassifier_b_kernel(tc, x, wp, bp, ws, bs, wc, bc, cw, of
     ):
         x_sb = {}
 
+        def columns(b):
+            return slice(FIRST[b], FIRST[b] + WIDTHS[b])
+
         def load_x_piece(b, g):
             ks = slice(g * KG, (g + 1) * KG)
-            nc.sync.dma_start(x_sb[b][:, ks, :], x_view[:, ks, b * BW : (b + 1) * BW])
+            nc.sync.dma_start(x_sb[b][:, ks, :], x_view[:, ks, columns(b)])
 
         def load_x(b):
-            x_sb[b] = xs.tile([P, KC, BW], BF16, name="x_sb")
+            x_sb[b] = xs.tile([P, KC, WIDTHS[b]], BF16, name="x_sb")
             for g in range(KC // KG):
                 load_x_piece(b, g)
 
@@ -67,7 +72,7 @@ def tile_jointembeddingclassifier_b_kernel(tc, x, wp, bp, ws, bs, wc, bc, cw, of
 
         for m in range(NCHILD // 2):
             load_cw(child_of(m))
-        x_sb[1] = xs.tile([P, KC, BW], BF16, name="x_sb")
+        x_sb[1] = xs.tile([P, KC, WIDTHS[1]], BF16, name="x_sb")
         for g in range(KC // KG):
             load_x_piece(1, g)
             load_cw(child_of(NCHILD // 2 + g))
@@ -93,43 +98,41 @@ def tile_jointembeddingclassifier_b_kernel(tc, x, wp, bp, ws, bs, wc, bc, cw, of
         hs_sb, hp_bf, q, q_bf = {}, {}, {}, {}
 
         def project(acc_pool, name, w_sb, b):
-            ps = acc_pool.tile([P, BW], FP32, name=name)
+            ps = acc_pool.tile([P, WIDTHS[b]], FP32, name=name)
             for k in range(KC):
                 nc.tensor.matmul(ps[:], w_sb[:, k, :], x_sb[b][:, k, :], start=(k == 0), stop=(k == KC - 1))
             return ps
 
         def child_projection(b):
-            cols = slice(b * BW, (b + 1) * BW)
             hs_ps = project(hs_acc, "hs_ps", ws_sb, b)
-            hs_sb[b] = acts.tile([P, BW], FP32, name="hs_sb")
+            hs_sb[b] = acts.tile([P, WIDTHS[b]], FP32, name="hs_sb")
             nc.scalar.activation(hs_sb[b][:], hs_ps[:], IDENTITY, bias=bs_sb[:])
-            nc.sync.dma_start(out[ROW_HS : ROW_HS + D, cols], hs_sb[b][:])
+            nc.sync.dma_start(out[ROW_HS : ROW_HS + D, columns(b)], hs_sb[b][:])
 
         def parent_projection(b):
-            cols = slice(b * BW, (b + 1) * BW)
             hp_ps = project(hp_acc, "hp_ps", wp_sb, b)
-            hp_bf[b] = acts.tile([P, BW], BF16, name="hp_bf")
+            hp_bf[b] = acts.tile([P, WIDTHS[b]], BF16, name="hp_bf")
             nc.scalar.activation(hp_bf[b][:], hp_ps[:], IDENTITY, bias=bp_sb[:])
-            hp_sb = acts.tile([P, BW], FP32, name="hp_sb")
+            hp_sb = acts.tile([P, WIDTHS[b]], FP32, name="hp_sb")
             nc.scalar.activation(hp_sb[:], hp_ps[:], IDENTITY, bias=bp_sb[:])
-            nc.sync.dma_start(out[ROW_HP : ROW_HP + D, cols], hp_sb[:])
+            nc.sync.dma_start(out[ROW_HP : ROW_HP + D, columns(b)], hp_sb[:])
 
         def look_up(b):
-            q[b] = prods.tile([P, NCHILD, BW], FP32, name="q")
-            block_offsets = offsets[:, b * (BW // 16) : (b + 1) * (BW // 16)]
+            q[b] = prods.tile([P, NCHILD, WIDTHS[b]], FP32, name="q")
+            block_offsets = offsets[:, FIRST[b] // 16 : (FIRST[b] + WIDTHS[b]) // 16]
             for m in range(NCHILD):
                 window = cw_sb[child_of(m)]
                 nc.vector.tensor_tensor(q[b][:, m, :], window[:].indirect(block_offsets), hs_sb[b][:], MULT)
 
         def round_products(engine_copy, name, b, s):
-            q_bf[b, s] = rounded.tile([P, NT, BW], BF16, name=name)
+            q_bf[b, s] = rounded.tile([P, NT, WIDTHS[b]], BF16, name=name)
             for t in range(0, NT, 2):
                 engine_copy(q_bf[b, s][:, t : t + 2, :], q[b][:, NT * s + t : NT * s + t + 2, :])
 
         def sum_products(b, s):
-            for h in range(b * BW // HW, (b + 1) * BW // HW):
+            for h in range(FIRST[b] // HW, (FIRST[b] + WIDTHS[b]) // HW):
                 r = NH * s + h
-                first = h * HW - b * BW
+                first = h * HW - FIRST[b]
                 for t in range(NT):
                     nc.tensor.matmul(
                         lc_ps[QUAD * t : QUAD * (t + 1), :],
@@ -140,16 +143,15 @@ def tile_jointembeddingclassifier_b_kernel(tc, x, wp, bp, ws, bs, wc, bc, cw, of
                     )
 
         def parent_logits(b):
-            cols = slice(b * BW, (b + 1) * BW)
             for c in range(SC):
-                lp_ps = lp_acc.tile([P, BW], FP32, name="lp_ps")
+                lp_ps = lp_acc.tile([P, WIDTHS[b]], FP32, name="lp_ps")
                 nc.tensor.matmul(lp_ps[:], wc_sb[:, c * P : (c + 1) * P], hp_bf[b][:], start=True, stop=True)
-                lp_sb = lps.tile([P, BW], FP32, name="lp_sb")
+                lp_sb = lps.tile([P, WIDTHS[b]], FP32, name="lp_sb")
                 if b == LAST and c % 2 == 1:
                     nc.vector.tensor_scalar_add(lp_sb[:], lp_ps[:], bc_sb[c][:])
                 else:
                     nc.scalar.activation(lp_sb[:], lp_ps[:], IDENTITY, bias=bc_sb[c][:])
-                nc.sync.dma_start(out[c * P : (c + 1) * P, cols], lp_sb[:])
+                nc.sync.dma_start(out[c * P : (c + 1) * P, columns(b)], lp_sb[:])
 
         for i in range(NB + 2):
             if i + 2 < NB:

@@ -31,10 +31,10 @@ def tile_jointembeddingclassifier_b_kernel(tc, x, wp, bp, ws, bs, wc, bc, cw, of
     x_view = x.rearrange("(p k) j -> p k j", k=KC)
     with (
         tc.tile_pool(name="held", bufs=1) as held,
-        tc.tile_pool(name="xs", bufs=4) as xs,
-        tc.tile_pool(name="acts", bufs=3) as acts,
+        tc.tile_pool(name="xs", bufs=5) as xs,
+        tc.tile_pool(name="acts", bufs=4) as acts,
         tc.tile_pool(name="lps", bufs=8) as lps,
-        tc.tile_pool(name="prods", bufs=2) as prods,
+        tc.tile_pool(name="prods", bufs=3) as prods,
         tc.tile_pool(name="rounded", bufs=1) as rounded,
         tc.psum_pool(name="hs_acc", bufs=2) as hs_acc,
         tc.psum_pool(name="hp_acc", bufs=1) as hp_acc,
@@ -76,6 +76,7 @@ def tile_jointembeddingclassifier_b_kernel(tc, x, wp, bp, ws, bs, wc, bc, cw, of
         for g in range(KC // KG):
             load_x_piece(1, g)
             load_cw(child_of(NCHILD // 2 + g))
+        load_x(2)
 
         bs_sb = held.tile([P, 1], FP32, name="bs_sb")
         nc.scalar.dma_start(bs_sb[:], bs)
@@ -154,8 +155,8 @@ def tile_jointembeddingclassifier_b_kernel(tc, x, wp, bp, ws, bs, wc, bc, cw, of
                 nc.sync.dma_start(out[c * P : (c + 1) * P, columns(b)], lp_sb[:])
 
         for i in range(NB + 2):
-            if i + 2 < NB:
-                load_x(i + 2)
+            if i + 3 < NB:
+                load_x(i + 3)
             if i < NB:
                 child_projection(i)
             if 2 <= i:

@@ -20,6 +20,8 @@ WIDTHS = [BW] * (N // BW - 1) + [HW, HW]
 FIRST = [sum(WIDTHS[:b]) for b in range(len(WIDTHS))]
 NB = len(WIDTHS)
 LAST = NB - 1
+X_WIDTHS = [BW] * (N // BW // 2) + [2 * BW] * (N // BW // 4)
+X_FIRST = [sum(X_WIDTHS[:a]) for a in range(len(X_WIDTHS))]
 
 ROW_LC, ROW_HP, ROW_HS = S, S + NCHILD, S + NCHILD + D
 
@@ -31,7 +33,8 @@ def tile_jointembeddingclassifier_b_kernel(tc, x, wp, bp, ws, bs, wc, bc, cw, of
     x_view = x.rearrange("(p k) j -> p k j", k=KC)
     with (
         tc.tile_pool(name="held", bufs=1) as held,
-        tc.tile_pool(name="xs", bufs=5) as xs,
+        tc.tile_pool(name="xs", bufs=3) as xs,
+        tc.tile_pool(name="wide_xs", bufs=2) as wide_xs,
         tc.tile_pool(name="acts", bufs=4) as acts,
         tc.tile_pool(name="lps", bufs=8) as lps,
         tc.tile_pool(name="prods", bufs=3) as prods,
@@ -46,18 +49,30 @@ def tile_jointembeddingclassifier_b_kernel(tc, x, wp, bp, ws, bs, wc, bc, cw, of
         def columns(b):
             return slice(FIRST[b], FIRST[b] + WIDTHS[b])
 
-        def load_x_piece(b, g):
+        def load_x_piece(a, g):
             ks = slice(g * KG, (g + 1) * KG)
-            nc.sync.dma_start(x_sb[b][:, ks, :], x_view[:, ks, columns(b)])
+            nc.sync.dma_start(x_sb[a][:, ks, :], x_view[:, ks, X_FIRST[a] : X_FIRST[a] + X_WIDTHS[a]])
 
-        def load_x(b):
-            x_sb[b] = xs.tile([P, KC, WIDTHS[b]], BF16, name="x_sb")
-            for g in range(KC // KG):
-                load_x_piece(b, g)
+        def new_x_tile(a):
+            if X_WIDTHS[a] == BW:
+                x_sb[a] = xs.tile([P, KC, BW], BF16, name="x_sb")
+            else:
+                x_sb[a] = wide_xs.tile([P, KC, 2 * BW], BF16, name="x_wide")
+
+        def load_x_from(b):
+            if FIRST[b] in X_FIRST:
+                a = X_FIRST.index(FIRST[b])
+                new_x_tile(a)
+                for g in range(KC // KG):
+                    load_x_piece(a, g)
+
+        def x_chunk(b, k):
+            a = max(i for i in range(len(X_FIRST)) if X_FIRST[i] <= FIRST[b])
+            return x_sb[a][:, k, FIRST[b] - X_FIRST[a] : FIRST[b] - X_FIRST[a] + WIDTHS[b]]
 
         ws_sb = held.tile([P, KC, D], BF16, name="ws_sb")
         nc.sync.dma_start(ws_sb[:], ws.rearrange("(p k) d -> p k d", k=KC))
-        load_x(0)
+        load_x_from(0)
         offsets = held.tile([P, N // 16], U16, name="offsets")
         nc.sync.dma_start(offsets[:], offs)
         wp_sb = held.tile([P, KC, D], BF16, name="wp_sb")
@@ -72,11 +87,11 @@ def tile_jointembeddingclassifier_b_kernel(tc, x, wp, bp, ws, bs, wc, bc, cw, of
 
         for m in range(NCHILD // 2):
             load_cw(child_of(m))
-        x_sb[1] = xs.tile([P, KC, WIDTHS[1]], BF16, name="x_sb")
+        new_x_tile(1)
         for g in range(KC // KG):
             load_x_piece(1, g)
             load_cw(child_of(NCHILD // 2 + g))
-        load_x(2)
+        load_x_from(2)
 
         bs_sb = held.tile([P, 1], FP32, name="bs_sb")
         nc.scalar.dma_start(bs_sb[:], bs)
@@ -101,7 +116,7 @@ def tile_jointembeddingclassifier_b_kernel(tc, x, wp, bp, ws, bs, wc, bc, cw, of
         def project(acc_pool, name, w_sb, b):
             ps = acc_pool.tile([P, WIDTHS[b]], FP32, name=name)
             for k in range(KC):
-                nc.tensor.matmul(ps[:], w_sb[:, k, :], x_sb[b][:, k, :], start=(k == 0), stop=(k == KC - 1))
+                nc.tensor.matmul(ps[:], w_sb[:, k, :], x_chunk(b, k), start=(k == 0), stop=(k == KC - 1))
             return ps
 
         def child_projection(b):
@@ -156,7 +171,7 @@ def tile_jointembeddingclassifier_b_kernel(tc, x, wp, bp, ws, bs, wc, bc, cw, of
 
         for i in range(NB + 2):
             if i + 3 < NB:
-                load_x(i + 3)
+                load_x_from(i + 3)
             if i < NB:
                 child_projection(i)
             if 2 <= i:

import concourse.mybir as mybir

FP32 = mybir.dt.float32
BF16 = mybir.dt.bfloat16
U16 = mybir.dt.uint16
MULT = mybir.AluOpType.mult
IDENTITY = mybir.ActivationFunctionType.Identity

P = 128
DIN, D, NCHILD, S, N = 2048, 128, 8, 512, 4096
KC = DIN // P
KG = 4
BW = 512
SC = S // P
QUAD = 32
NT = P // QUAD
HW = N * NCHILD // P
NH = N // HW
WIDTHS = [BW] * (N // BW - 1) + [HW, HW]
FIRST = [sum(WIDTHS[:b]) for b in range(len(WIDTHS))]
NB = len(WIDTHS)
LAST = NB - 1
X_WIDTHS = [BW] * (N // BW // 2) + [2 * BW] * (N // BW // 4)
X_FIRST = [sum(X_WIDTHS[:a]) for a in range(len(X_WIDTHS))]

ROW_LC, ROW_HP, ROW_HS = S, S + NCHILD, S + NCHILD + D

FLOPS = 2 * DIN * 2 * D * N + 2 * D * S * N + 2 * NCHILD * D * N


def tile_jointembeddingclassifier_b_kernel(tc, x, wp, bp, ws, bs, wc, bc, cw, offs, out):
    nc = tc.nc
    x_view = x.rearrange("(p k) j -> p k j", k=KC)
    with (
        tc.tile_pool(name="held", bufs=1) as held,
        tc.tile_pool(name="xs", bufs=3) as xs,
        tc.tile_pool(name="wide_xs", bufs=2) as wide_xs,
        tc.tile_pool(name="acts", bufs=4) as acts,
        tc.tile_pool(name="lps", bufs=8) as lps,
        tc.tile_pool(name="prods", bufs=3) as prods,
        tc.tile_pool(name="rounded", bufs=1) as rounded,
        tc.psum_pool(name="hs_acc", bufs=2) as hs_acc,
        tc.psum_pool(name="hp_acc", bufs=1) as hp_acc,
        tc.psum_pool(name="lp_acc", bufs=4) as lp_acc,
        tc.psum_pool(name="lc_acc", bufs=1) as lc_acc,
    ):
        x_sb = {}

        def columns(b):
            return slice(FIRST[b], FIRST[b] + WIDTHS[b])

        def load_x_piece(a, g):
            ks = slice(g * KG, (g + 1) * KG)
            nc.sync.dma_start(x_sb[a][:, ks, :], x_view[:, ks, X_FIRST[a] : X_FIRST[a] + X_WIDTHS[a]])

        def new_x_tile(a):
            if X_WIDTHS[a] == BW:
                x_sb[a] = xs.tile([P, KC, BW], BF16, name="x_sb")
            else:
                x_sb[a] = wide_xs.tile([P, KC, 2 * BW], BF16, name="x_wide")

        def load_x_from(b):
            if FIRST[b] in X_FIRST:
                a = X_FIRST.index(FIRST[b])
                new_x_tile(a)
                for g in range(KC // KG):
                    load_x_piece(a, g)

        def x_chunk(b, k):
            a = max(i for i in range(len(X_FIRST)) if X_FIRST[i] <= FIRST[b])
            return x_sb[a][:, k, FIRST[b] - X_FIRST[a] : FIRST[b] - X_FIRST[a] + WIDTHS[b]]

        ws_sb = held.tile([P, KC, D], BF16, name="ws_sb")
        nc.sync.dma_start(ws_sb[:], ws.rearrange("(p k) d -> p k d", k=KC))
        load_x_from(0)
        offsets = held.tile([P, N // 16], U16, name="offsets")
        nc.sync.dma_start(offsets[:], offs)
        wp_sb = held.tile([P, KC, D], BF16, name="wp_sb")
        nc.sync.dma_start(wp_sb[:], wp.rearrange("(p k) d -> p k d", k=KC))
        cw_sb = [held.tile([P, S], FP32, name=f"cw{n}") for n in range(NCHILD)]

        def child_of(m):
            return 2 * (m % NT) + m // NT

        def load_cw(n):
            nc.sync.dma_start(cw_sb[n][:], cw[n * P : (n + 1) * P, :])

        for m in range(NCHILD // 2):
            load_cw(child_of(m))
        new_x_tile(1)
        for g in range(KC // KG):
            load_x_piece(1, g)
            load_cw(child_of(NCHILD // 2 + g))
        load_x_from(2)

        bs_sb = held.tile([P, 1], FP32, name="bs_sb")
        nc.scalar.dma_start(bs_sb[:], bs)
        bp_sb = held.tile([P, 1], FP32, name="bp_sb")
        nc.scalar.dma_start(bp_sb[:], bp)
        wc_sb = held.tile([P, S], BF16, name="wc_sb")
        nc.scalar.dma_start(wc_sb[:], wc)
        bc_sb = []
        for c in range(SC):
            bias = held.tile([P, 1], FP32, name=f"bc{c}")
            nc.scalar.dma_start(bias[:], bc[c * P : (c + 1) * P, :])
            bc_sb.append(bias)

        strip = held.tile([P, 2 * QUAD - 1], BF16, name="strip")
        nc.vector.memset(strip[:], 0.0)
        nc.vector.memset(strip[:, QUAD - 1 : QUAD], 1.0)

        lc_ps = lc_acc.tile([P, HW], FP32, name="lc_ps")

        hs_sb, hp_bf, q, q_bf = {}, {}, {}, {}

        def project(acc_pool, name, w_sb, b):
            ps = acc_pool.tile([P, WIDTHS[b]], FP32, name=name)
            for k in range(KC):
                nc.tensor.matmul(ps[:], w_sb[:, k, :], x_chunk(b, k), start=(k == 0), stop=(k == KC - 1))
            return ps

        def child_projection(b):
            hs_ps = project(hs_acc, "hs_ps", ws_sb, b)
            hs_sb[b] = acts.tile([P, WIDTHS[b]], FP32, name="hs_sb")
            nc.scalar.activation(hs_sb[b][:], hs_ps[:], IDENTITY, bias=bs_sb[:])
            nc.sync.dma_start(out[ROW_HS : ROW_HS + D, columns(b)], hs_sb[b][:])

        def parent_projection(b):
            hp_ps = project(hp_acc, "hp_ps", wp_sb, b)
            hp_bf[b] = acts.tile([P, WIDTHS[b]], BF16, name="hp_bf")
            nc.scalar.activation(hp_bf[b][:], hp_ps[:], IDENTITY, bias=bp_sb[:])
            hp_sb = acts.tile([P, WIDTHS[b]], FP32, name="hp_sb")
            nc.scalar.activation(hp_sb[:], hp_ps[:], IDENTITY, bias=bp_sb[:])
            nc.sync.dma_start(out[ROW_HP : ROW_HP + D, columns(b)], hp_sb[:])

        def look_up(b):
            q[b] = prods.tile([P, NCHILD, WIDTHS[b]], FP32, name="q")
            block_offsets = offsets[:, FIRST[b] // 16 : (FIRST[b] + WIDTHS[b]) // 16]
            for m in range(NCHILD):
                window = cw_sb[child_of(m)]
                nc.vector.tensor_tensor(q[b][:, m, :], window[:].indirect(block_offsets), hs_sb[b][:], MULT)

        def round_products(engine_copy, name, b, s):
            q_bf[b, s] = rounded.tile([P, NT, WIDTHS[b]], BF16, name=name)
            for t in range(0, NT, 2):
                engine_copy(q_bf[b, s][:, t : t + 2, :], q[b][:, NT * s + t : NT * s + t + 2, :])

        def sum_products(b, s):
            for h in range(FIRST[b] // HW, (FIRST[b] + WIDTHS[b]) // HW):
                r = NH * s + h
                first = h * HW - FIRST[b]
                for t in range(NT):
                    nc.tensor.matmul(
                        lc_ps[QUAD * t : QUAD * (t + 1), :],
                        strip[:, QUAD - 1 - r : 2 * QUAD - 1 - r],
                        q_bf[b, s][:, t, first : first + HW],
                        start=(r == 0),
                        stop=(r == QUAD - 1),
                    )

        def parent_logits(b):
            for c in range(SC):
                lp_ps = lp_acc.tile([P, WIDTHS[b]], FP32, name="lp_ps")
                nc.tensor.matmul(lp_ps[:], wc_sb[:, c * P : (c + 1) * P], hp_bf[b][:], start=True, stop=True)
                lp_sb = lps.tile([P, WIDTHS[b]], FP32, name="lp_sb")
                if b == LAST and c % 2 == 1:
                    nc.vector.tensor_scalar_add(lp_sb[:], lp_ps[:], bc_sb[c][:])
                else:
                    nc.scalar.activation(lp_sb[:], lp_ps[:], IDENTITY, bias=bc_sb[c][:])
                nc.sync.dma_start(out[c * P : (c + 1) * P, columns(b)], lp_sb[:])

        for i in range(NB + 2):
            if i + 3 < NB:
                load_x_from(i + 3)
            if i < NB:
                child_projection(i)
            if 2 <= i:
                sum_products(i - 2, 0)
            if 1 <= i <= LAST:
                round_products(nc.scalar.copy, "q_bf_lower", i - 1, 0)
            if 2 <= i:
                parent_logits(i - 2)
            if i < NB:
                look_up(i)
            if i == LAST:
                round_products(nc.vector.tensor_copy, "q_bf_lower_last", LAST, 0)
                round_products(nc.vector.tensor_copy, "q_bf_upper_last", LAST, 1)
            if 1 <= i <= NB:
                parent_projection(i - 1)
            if 2 <= i:
                sum_products(i - 2, 1)
            if 1 <= i <= LAST:
                round_products(nc.scalar.copy, "q_bf_upper", i - 1, 1)

        lc_sb = held.tile([P, HW], FP32, name="lc_sb")
        nc.scalar.copy(lc_sb[:], lc_ps[:])
        nc.sync.dma_start(out[ROW_LC : ROW_LC + NCHILD, :].rearrange("n (h j) -> (n h) j", j=HW), lc_sb[:])
